import numpy as np
import ml_dtypes


def mxq(x, axis, fmt="e4m3"):
    dtype, down = {"e4m3": (ml_dtypes.float8_e4m3fn, 7), "e5m2": (ml_dtypes.float8_e5m2, 14)}[fmt]
    v = np.moveaxis(np.asarray(x, np.float32).astype(ml_dtypes.bfloat16).astype(np.float64), axis, -1)
    blocks = v.reshape(v.shape[:-1] + (-1, 32))
    amax = np.abs(blocks).max(-1, keepdims=True)
    byte = np.maximum(np.where(amax > 0, np.frexp(amax)[1] - 1 + 127, 0) - down, 1)
    scale = np.exp2(byte - 127.0)
    codes = (blocks / scale).astype(np.float32).astype(dtype).astype(np.float64)
    return np.moveaxis((codes * scale).reshape(v.shape), -1, axis)


WIDE = False


def mx_kscale(k):
    if not WIDE:
        return np.ones(k)
    levels = np.array([10, -10, 5, -5, 0])
    a = np.random.permutation(np.resize(levels, k // 512 * 4)).reshape(k // 512, 4)
    idx = np.arange(k)
    return np.exp2(a[idx // 512, idx % 128 // 32])


BF16 = ml_dtypes.bfloat16


def bf(x):
    return np.asarray(x, np.float32).astype(BF16)


def f64(x):
    return np.asarray(x).astype(np.float64)


E2M1 = np.array([0.0, 0.5, 1.0, 1.5, 2.0, 3.0, 4.0, 6.0, -0.0, -0.5, -1.0, -1.5, -2.0, -3.0, -4.0, -6.0])


def pack_weight(w, fmt):
    k, n = w.shape
    w = f64(bf(w)).reshape(k // 32, 32, n)
    amax = np.abs(w).max(1)
    if fmt == "e4m3":
        byte = np.frexp(amax)[1] - 1 + 127 - 7
    else:
        mant, ex = np.frexp(amax / 6.0)
        byte = np.where(mant > 0.5, ex, ex - 1) + 127
    byte = np.clip(np.where(amax > 0, byte, 1), 1, 254)
    scaled = (w * np.exp2(127.0 - byte)[:, None, :]).reshape(k, n).astype(np.float32)
    by_word = np.ascontiguousarray(scaled.reshape(k // 512, 128, 4, n).transpose(0, 1, 3, 2))
    if fmt == "e4m3":
        words = by_word.astype(ml_dtypes.float8_e4m3fn).view(np.uint8)
    else:
        c = by_word.astype(ml_dtypes.float4_e2m1fn).view(np.uint8) & 0xF
        words = c[..., 0::2] | (c[..., 1::2] << 4)
    return np.ascontiguousarray(words), np.ascontiguousarray(byte.astype(np.uint8).reshape(k // 512, 16, n))


def unpack_weight(words, scales, fmt):
    g, p, n, _ = words.shape
    if fmt == "e4m3":
        vals = np.ascontiguousarray(words).view(ml_dtypes.float8_e4m3fn).astype(np.float64)
    else:
        nib = np.empty((g, p, n, 4), np.uint8)
        nib[..., 0::2] = words & 0xF
        nib[..., 1::2] = words >> 4
        vals = E2M1[nib]
    vals = vals * np.repeat(np.exp2(scales.astype(np.float64) - 127.0), 8, axis=1)[..., None]
    return vals.transpose(0, 1, 3, 2).reshape(g * 512, n)


B, H, N, D, DT, NH = 32, 128, 128, 1024, 1024, 8


def softmax(v, axis):
    e = np.exp(v - v.max(axis=axis, keepdims=True))
    return e / e.sum(axis=axis, keepdims=True)


def setup_inputs():
    s = mx_kscale(DT)
    cand_topics = bf(np.random.standard_normal((B, N, DT)) * s)
    Wq = np.random.standard_normal((D, DT)) * 2.0 / np.sqrt(DT) / s[None, :]
    Wq_words, Wq_scales = pack_weight(np.ascontiguousarray(Wq.T), "e4m3")
    bq = bf(np.random.standard_normal(D) * 0.5)
    return {"cand_topics": cand_topics,
            "Wq_words": Wq_words,
            "Wq_scales": Wq_scales,
            "bq": bq}


def reference(cand_topics, Wq_words, Wq_scales, bq):
    q = (mxq(f64(cand_topics), 2, "e4m3") @ unpack_weight(Wq_words, Wq_scales, "e4m3")) + f64(bq)
    query_weights = softmax(np.sqrt((q ** 2).sum(axis=-1)), 1)
    return q, query_weights

@@ -1,0 +1,191 @@
+from contextlib import ExitStack
+
+import concourse.mybir as mybir
+from concourse.masks import make_identity
+
+F32 = mybir.dt.float32
+BF16 = mybir.dt.bfloat16
+I32 = mybir.dt.int32
+U32 = mybir.dt.uint32
+U8 = mybir.dt.uint8
+FP8X4 = mybir.dt.float8_e4m3fn_x4
+ACT = mybir.ActivationFunctionType
+ALU = mybir.AluOpType
+AXIS = mybir.AxisListType
+
+P = 128
+USERS = 32
+D_IN = 1024
+D_OUT = 1024
+PACK = 4
+K_PASS = P * PACK
+PASSES = D_IN // K_PASS
+WORDS_PER_PASS = K_PASS // 2
+PLANES = 2
+BANK = 512
+HALVES = D_OUT // BANK
+PSUM_BANKS = 8
+
+ROUND = 2
+VECTOR_COPY_EVERY = 4
+Q_BUFS = 12
+
+FLOPS = 2 * USERS * P * D_IN * D_OUT
+
+
+def tile_candidateaware_clickednewsattention_pa_t_kernel(
+    tc, cand_topics, Wq_words, Wq_scales, bq, out_0, out_1
+):
+    nc = tc.nc
+    with ExitStack() as ctx:
+        ctx.enter_context(tc.manual_schedule())
+        consts = ctx.enter_context(tc.tile_pool(name="consts", bufs=1))
+        x_pool = ctx.enter_context(tc.tile_pool(name="x_pool", bufs=1))
+        mx_pool = ctx.enter_context(tc.tile_pool(name="mx_pool", bufs=2 * ROUND))
+        q_pool = ctx.enter_context(tc.tile_pool(name="q_pool", bufs=Q_BUFS))
+        xt_psum = ctx.enter_context(tc.psum_pool(name="xt_psum", bufs=ROUND))
+        acc_psum = ctx.enter_context(tc.psum_pool(name="acc_psum", bufs=PSUM_BANKS - ROUND))
+
+        bias_row = consts.tile([P, D_OUT], BF16)
+        nc.vector.memset(bias_row[:], 0.0)
+        w_scales = consts.tile([P, PASSES, D_OUT], U8, align_bytes=64)
+        nc.vector.memset(w_scales[:].bitcast(I32), 0)
+        ones = consts.tile([P, P], BF16)
+        nc.vector.memset(ones[:], 1.0)
+        square_sums = consts.tile([P, P], F32)
+        nc.vector.memset(square_sums[:], 0.0)
+        table_warmer = consts.tile([P, 1], F32)
+        nc.vector.memset(table_warmer[:], 1.0)
+        identity = consts.tile([P, P], F32)
+        make_identity(nc, identity[:])
+
+        nc.scalar.activation(out=table_warmer[:], in_=table_warmer[:], func=ACT.Sqrt)
+
+        nc.scalar.dma_start(out=bias_row[0:1, :], in_=bq.rearrange("(o d) -> o d", o=1))
+
+        x_tiles = []
+        for b in range(USERS):
+            x_tile = x_pool.tile([P, D_IN], BF16, name="x_tile%d" % b)
+            x_tiles.append(x_tile)
+
+        def load_x(b):
+            nc.sync.dma_start(out=x_tiles[b][:], in_=cand_topics[b])
+
+        for b in range(2 * ROUND):
+            load_x(b)
+        for quadrant in range(4):
+            nc.sync.dma_start(
+                out=w_scales[32 * quadrant : 32 * quadrant + 4, :, :].bitcast(I32),
+                in_=Wq_scales[:, 4 * quadrant : 4 * quadrant + 4, :]
+                .rearrange("g r n -> r g n")
+                .bitcast(I32),
+            )
+        w_codes = consts.tile([P, PASSES, PACK * D_OUT], U8, align_bytes=64)
+        w_bytes = Wq_words.rearrange("g p n t -> p g (n t)")
+        for h in range(HALVES):
+            half_bytes = slice(PACK * BANK * h, PACK * BANK * (h + 1))
+            nc.sync.dma_start(
+                out=w_codes[:, :, half_bytes].bitcast(I32),
+                in_=w_bytes[:, :, half_bytes].bitcast(I32),
+            )
+        for b in range(2 * ROUND, USERS):
+            load_x(b)
+
+        bias = consts.tile([P, D_OUT], F32)
+        for h in range(HALVES):
+            acc = acc_psum.tile([P, BANK], F32)
+            nc.tensor.matmul(
+                out=acc[:], lhsT=ones[:], rhs=bias_row[:, BANK * h : BANK * (h + 1)], start=True, stop=True
+            )
+            nc.vector.tensor_copy(out=bias[:, BANK * h : BANK * (h + 1)], in_=acc[:])
+
+        grouped_tiles = {}
+        x_operands = {}
+        q_tiles = {}
+
+        def transpose_tile(b):
+            words = x_tiles[b][:].bitcast(F32)
+            xt = xt_psum.tile([P, PASSES, PLANES, P], F32)
+            for g in range(PASSES):
+                for u in range(PLANES):
+                    nc.tensor.transpose(
+                        xt[:, g, u, :],
+                        words[:, WORDS_PER_PASS * g + u : WORDS_PER_PASS * (g + 1) : PLANES],
+                        identity[:],
+                    )
+            grouped = mx_pool.tile([P, PASSES, P, PACK], BF16, align_bytes=64)
+            planes_side_by_side = xt[:].rearrange("p g u n -> p g n u")
+            if b % VECTOR_COPY_EVERY == VECTOR_COPY_EVERY - 1:
+                nc.vector.tensor_copy(out=grouped[:].bitcast(F32), in_=planes_side_by_side)
+            else:
+                nc.scalar.copy(out=grouped[:].bitcast(F32), in_=planes_side_by_side)
+            grouped_tiles[b] = grouped
+
+        def quantise_tile(b):
+            x_codes = mx_pool.tile([P, PASSES * P], U32, align_bytes=64)
+            x_scales = mx_pool.tile([P, PASSES * P], U8, align_bytes=64)
+            nc.vector.quantize_mx(
+                out=x_codes[:].bitcast(FP8X4),
+                scales=x_scales[:],
+                in_=grouped_tiles[b][:].rearrange("p g n t -> p (g n t)"),
+            )
+            x_operands[b] = (x_codes, x_scales)
+
+        def project_tile(b):
+            x_codes, x_scales = x_operands[b]
+            q_tile = q_pool.tile([P, D_OUT], F32)
+            for h in range(HALVES):
+                acc = acc_psum.tile([P, BANK], F32)
+                for g in range(PASSES):
+                    nc.tensor.matmul_mx(
+                        out=acc[:],
+                        lhsT=x_codes[:, P * g : P * (g + 1)].bitcast(FP8X4),
+                        lhsT_scale=x_scales[:, P * g : P * (g + 1)],
+                        rhs=w_codes[:, g, PACK * BANK * h : PACK * BANK * (h + 1)].bitcast(FP8X4),
+                        rhs_scale=w_scales[:, g, BANK * h : BANK * (h + 1)],
+                        start=(g == 0),
+                        stop=(g == PASSES - 1),
+                    )
+                features = slice(BANK * h, BANK * (h + 1))
+                nc.vector.tensor_tensor(out=q_tile[:, features], in0=acc[:], in1=bias[:, features], op=ALU.add)
+            nc.sync.dma_start(out=out_0[b], in_=q_tile[:])
+            q_tiles[b] = q_tile
+
+        squares = consts.tile([P, D_OUT], F32)
+
+        def sum_squares(b):
+            nc.scalar.activation(
+                out=squares[:], in_=q_tiles[b][:], func=ACT.Square, accum_out=square_sums[:, b : b + 1]
+            )
+
+        for b in range(ROUND):
+            transpose_tile(b)
+        for b in range(ROUND):
+            quantise_tile(b)
+        for first in range(0, USERS, ROUND):
+            for b in range(first + ROUND, min(first + 2 * ROUND, USERS)):
+                transpose_tile(b)
+            for b in range(first, first + ROUND):
+                project_tile(b)
+                if b > 0:
+                    sum_squares(b - 1)
+                if b + ROUND < USERS:
+                    quantise_tile(b + ROUND)
+        sum_squares(USERS - 1)
+
+        sums_by_user = xt_psum.tile([P, P], F32, tag="xt")
+        nc.tensor.transpose(sums_by_user[:], square_sums[:], identity[:])
+        norms = consts.tile([P, P], F32)
+        nc.scalar.activation(out=norms[:USERS], in_=sums_by_user[:USERS], func=ACT.Sqrt)
+        minus_max = consts.tile([P, 1], F32)
+        nc.vector.tensor_reduce(out=minus_max[:USERS], in_=norms[:USERS], axis=AXIS.X, op=ALU.max, negate=True)
+        exps = consts.tile([P, P], F32)
+        exp_sum = consts.tile([P, 1], F32)
+        nc.scalar.activation(
+            out=exps[:USERS], in_=norms[:USERS], func=ACT.Exp, bias=minus_max[:USERS], accum_out=exp_sum[:USERS]
+        )
+        one_over_sum = consts.tile([P, 1], F32)
+        nc.vector.reciprocal(out=one_over_sum[:USERS], in_=exp_sum[:USERS])
+        query_weights = consts.tile([P, P], F32)
+        nc.vector.tensor_scalar_mul(out=query_weights[:USERS], in0=exps[:USERS], scalar1=one_over_sum[:USERS])
+        nc.sync.dma_start(out=out_1, in_=query_weights[:USERS])

@@ -52,16 +52,18 @@ def tile_candidateaware_clickednewsattention_pa_t_kernel(
         nc.vector.memset(w_scales[:].bitcast(I32), 0)
         ones = consts.tile([P, P], BF16)
         nc.vector.memset(ones[:], 1.0)
-        square_sums = consts.tile([P, P], F32)
-        nc.vector.memset(square_sums[:], 0.0)
         table_warmer = consts.tile([P, 1], F32)
-        nc.vector.memset(table_warmer[:], 1.0)
+        nc.vector.memset(table_warmer[:], 0.0)
         identity = consts.tile([P, P], F32)
         make_identity(nc, identity[:])
-
-        nc.scalar.activation(out=table_warmer[:], in_=table_warmer[:], func=ACT.Sqrt)
+        norm_columns = consts.tile([P, P], F32)
+        nc.gpsimd.memset(norm_columns[:], 0.0)
+        one_half = consts.tile([P, 1], F32)
+        nc.gpsimd.memset(one_half[:], 0.5)
+        square_sums = consts.tile([P, USERS], F32)
 
         nc.scalar.dma_start(out=bias_row[0:1, :], in_=bq.rearrange("(o d) -> o d", o=1))
+        nc.scalar.activation(out=table_warmer[:], in_=table_warmer[:], func=ACT.Exp)
 
         x_tiles = []
         for b in range(USERS):
@@ -92,12 +94,14 @@ def tile_candidateaware_clickednewsattention_pa_t_kernel(
             load_x(b)
 
         bias = consts.tile([P, D_OUT], F32)
-        for h in range(HALVES):
-            acc = acc_psum.tile([P, BANK], F32)
-            nc.tensor.matmul(
-                out=acc[:], lhsT=ones[:], rhs=bias_row[:, BANK * h : BANK * (h + 1)], start=True, stop=True
-            )
-            nc.vector.tensor_copy(out=bias[:, BANK * h : BANK * (h + 1)], in_=acc[:])
+
+        def spread_bias():
+            for h in range(HALVES):
+                acc = acc_psum.tile([P, BANK], F32)
+                nc.tensor.matmul(
+                    out=acc[:], lhsT=ones[:], rhs=bias_row[:, BANK * h : BANK * (h + 1)], start=True, stop=True
+                )
+                nc.vector.tensor_copy(out=bias[:, BANK * h : BANK * (h + 1)], in_=acc[:])
 
         grouped_tiles = {}
         x_operands = {}
@@ -153,13 +157,17 @@ def tile_candidateaware_clickednewsattention_pa_t_kernel(
 
         squares = consts.tile([P, D_OUT], F32)
 
-        def sum_squares(b):
+        def norm_tile(b):
             nc.scalar.activation(
                 out=squares[:], in_=q_tiles[b][:], func=ACT.Square, accum_out=square_sums[:, b : b + 1]
+            )
+            nc.gpsimd.tensor_tensor(
+                out=norm_columns[:, b : b + 1], in0=square_sums[:, b : b + 1], in1=one_half[:], op=ALU.pow
             )
 
         for b in range(ROUND):
             transpose_tile(b)
+        spread_bias()
         for b in range(ROUND):
             quantise_tile(b)
         for first in range(0, USERS, ROUND):
@@ -168,15 +176,13 @@ def tile_candidateaware_clickednewsattention_pa_t_kernel(
             for b in range(first, first + ROUND):
                 project_tile(b)
                 if b > 0:
-                    sum_squares(b - 1)
+                    norm_tile(b - 1)
                 if b + ROUND < USERS:
                     quantise_tile(b + ROUND)
-        sum_squares(USERS - 1)
+        norm_tile(USERS - 1)
 
-        sums_by_user = xt_psum.tile([P, P], F32, tag="xt")
-        nc.tensor.transpose(sums_by_user[:], square_sums[:], identity[:])
-        norms = consts.tile([P, P], F32)
-        nc.scalar.activation(out=norms[:USERS], in_=sums_by_user[:USERS], func=ACT.Sqrt)
+        norms = xt_psum.tile([P, P], F32, tag="xt")
+        nc.tensor.transpose(norms[:], norm_columns[:], identity[:])
         minus_max = consts.tile([P, 1], F32)
         nc.vector.tensor_reduce(out=minus_max[:USERS], in_=norms[:USERS], axis=AXIS.X, op=ALU.max, negate=True)
         exps = consts.tile([P, P], F32)

@@ -20,15 +20,18 @@ D_OUT = 1024
 PACK = 4
 K_PASS = P * PACK
 PASSES = D_IN // K_PASS
-WORDS_PER_PASS = K_PASS // 2
-PLANES = 2
+PAIRS_PER_WORD = PACK // 2
+PAIRS_PER_PASS = K_PASS // 2
 BANK = 512
-HALVES = D_OUT // BANK
+BANKS_PER_USER = D_OUT // BANK
 PSUM_BANKS = 8
+QUADRANT = 32
+QUADRANTS = P // QUADRANT
+SCALE_ROWS = QUADRANT // 8
 
 ROUND = 2
 VECTOR_COPY_EVERY = 4
-Q_BUFS = 12
+Q_TILES = 16
 
 FLOPS = 2 * USERS * P * D_IN * D_OUT
 
@@ -42,7 +45,7 @@ def tile_candidateaware_clickednewsattention_pa_t_kernel(
         consts = ctx.enter_context(tc.tile_pool(name="consts", bufs=1))
         x_pool = ctx.enter_context(tc.tile_pool(name="x_pool", bufs=1))
         mx_pool = ctx.enter_context(tc.tile_pool(name="mx_pool", bufs=2 * ROUND))
-        q_pool = ctx.enter_context(tc.tile_pool(name="q_pool", bufs=Q_BUFS))
+        q_pool = ctx.enter_context(tc.tile_pool(name="q_pool", bufs=Q_TILES))
         xt_psum = ctx.enter_context(tc.psum_pool(name="xt_psum", bufs=ROUND))
         acc_psum = ctx.enter_context(tc.psum_pool(name="acc_psum", bufs=PSUM_BANKS - ROUND))
 
@@ -62,7 +65,7 @@ def tile_candidateaware_clickednewsattention_pa_t_kernel(
         nc.gpsimd.memset(one_half[:], 0.5)
         square_sums = consts.tile([P, USERS], F32)
 
-        nc.scalar.dma_start(out=bias_row[0:1, :], in_=bq.rearrange("(o d) -> o d", o=1))
+        nc.scalar.dma_start(out=bias_row[0:1, :], in_=bq.rearrange("(o f) -> o f", o=1))
         nc.scalar.activation(out=table_warmer[:], in_=table_warmer[:], func=ACT.Exp)
 
         x_tiles = []
@@ -75,20 +78,20 @@ def tile_candidateaware_clickednewsattention_pa_t_kernel(
 
         for b in range(2 * ROUND):
             load_x(b)
-        for quadrant in range(4):
+        for quadrant in range(QUADRANTS):
             nc.sync.dma_start(
-                out=w_scales[32 * quadrant : 32 * quadrant + 4, :, :].bitcast(I32),
-                in_=Wq_scales[:, 4 * quadrant : 4 * quadrant + 4, :]
-                .rearrange("g r n -> r g n")
+                out=w_scales[QUADRANT * quadrant : QUADRANT * quadrant + SCALE_ROWS, :, :].bitcast(I32),
+                in_=Wq_scales[:, SCALE_ROWS * quadrant : SCALE_ROWS * (quadrant + 1), :]
+                .rearrange("g r f -> r g f")
                 .bitcast(I32),
             )
         w_codes = consts.tile([P, PASSES, PACK * D_OUT], U8, align_bytes=64)
-        w_bytes = Wq_words.rearrange("g p n t -> p g (n t)")
-        for h in range(HALVES):
-            half_bytes = slice(PACK * BANK * h, PACK * BANK * (h + 1))
+        w_bytes = Wq_words.rearrange("g p f t -> p g (f t)")
+        for h in range(BANKS_PER_USER):
+            bank_bytes = slice(PACK * BANK * h, PACK * BANK * (h + 1))
             nc.sync.dma_start(
-                out=w_codes[:, :, half_bytes].bitcast(I32),
-                in_=w_bytes[:, :, half_bytes].bitcast(I32),
+                out=w_codes[:, :, bank_bytes].bitcast(I32),
+                in_=w_bytes[:, :, bank_bytes].bitcast(I32),
             )
         for b in range(2 * ROUND, USERS):
             load_x(b)
@@ -96,7 +99,7 @@ def tile_candidateaware_clickednewsattention_pa_t_kernel(
         bias = consts.tile([P, D_OUT], F32)
 
         def spread_bias():
-            for h in range(HALVES):
+            for h in range(BANKS_PER_USER):
                 acc = acc_psum.tile([P, BANK], F32)
                 nc.tensor.matmul(
                     out=acc[:], lhsT=ones[:], rhs=bias_row[:, BANK * h : BANK * (h + 1)], start=True, stop=True
@@ -108,21 +111,21 @@ def tile_candidateaware_clickednewsattention_pa_t_kernel(
         q_tiles = {}
 
         def transpose_tile(b):
-            words = x_tiles[b][:].bitcast(F32)
-            xt = xt_psum.tile([P, PASSES, PLANES, P], F32)
+            pairs = x_tiles[b][:].bitcast(F32)
+            xt = xt_psum.tile([P, PASSES, PAIRS_PER_WORD, P], F32)
             for g in range(PASSES):
-                for u in range(PLANES):
+                for u in range(PAIRS_PER_WORD):
                     nc.tensor.transpose(
                         xt[:, g, u, :],
-                        words[:, WORDS_PER_PASS * g + u : WORDS_PER_PASS * (g + 1) : PLANES],
+                        pairs[:, PAIRS_PER_PASS * g + u : PAIRS_PER_PASS * (g + 1) : PAIRS_PER_WORD],
                         identity[:],
                     )
             grouped = mx_pool.tile([P, PASSES, P, PACK], BF16, align_bytes=64)
-            planes_side_by_side = xt[:].rearrange("p g u n -> p g n u")
+            pairs_side_by_side = xt[:].rearrange("p g u n -> p g n u")
             if b % VECTOR_COPY_EVERY == VECTOR_COPY_EVERY - 1:
-                nc.vector.tensor_copy(out=grouped[:].bitcast(F32), in_=planes_side_by_side)
+                nc.vector.tensor_copy(out=grouped[:].bitcast(F32), in_=pairs_side_by_side)
             else:
-                nc.scalar.copy(out=grouped[:].bitcast(F32), in_=planes_side_by_side)
+                nc.scalar.copy(out=grouped[:].bitcast(F32), in_=pairs_side_by_side)
             grouped_tiles[b] = grouped
 
         def quantise_tile(b):
@@ -138,7 +141,7 @@ def tile_candidateaware_clickednewsattention_pa_t_kernel(
         def project_tile(b):
             x_codes, x_scales = x_operands[b]
             q_tile = q_pool.tile([P, D_OUT], F32)
-            for h in range(HALVES):
+            for h in range(BANKS_PER_USER):
                 acc = acc_psum.tile([P, BANK], F32)
                 for g in range(PASSES):
                     nc.tensor.matmul_mx(
@@ -167,18 +170,20 @@ def tile_candidateaware_clickednewsattention_pa_t_kernel(
 
         for b in range(ROUND):
             transpose_tile(b)
-        spread_bias()
         for b in range(ROUND):
             quantise_tile(b)
+        for b in range(ROUND, 2 * ROUND):
+            transpose_tile(b)
+        spread_bias()
         for first in range(0, USERS, ROUND):
-            for b in range(first + ROUND, min(first + 2 * ROUND, USERS)):
-                transpose_tile(b)
             for b in range(first, first + ROUND):
                 project_tile(b)
                 if b > 0:
                     norm_tile(b - 1)
                 if b + ROUND < USERS:
                     quantise_tile(b + ROUND)
+            for b in range(first + 2 * ROUND, min(first + 3 * ROUND, USERS)):
+                transpose_tile(b)
         norm_tile(USERS - 1)
 
         norms = xt_psum.tile([P, P], F32, tag="xt")

@@ -32,6 +32,7 @@ SCALE_ROWS = QUADRANT // 8
 ROUND = 2
 VECTOR_COPY_EVERY = 4
 Q_TILES = 16
+WARMING_MATMULS = 4
 
 FLOPS = 2 * USERS * P * D_IN * D_OUT
 
@@ -49,12 +50,14 @@ def tile_candidateaware_clickednewsattention_pa_t_kernel(
         xt_psum = ctx.enter_context(tc.psum_pool(name="xt_psum", bufs=ROUND))
         acc_psum = ctx.enter_context(tc.psum_pool(name="acc_psum", bufs=PSUM_BANKS - ROUND))
 
+        ones = consts.tile([P, P], BF16)
+        nc.vector.memset(ones[:], 1.0)
+        zeros = consts.tile([P, BANK], BF16)
+        nc.vector.memset(zeros[:], 0.0)
         bias_row = consts.tile([P, D_OUT], BF16)
         nc.vector.memset(bias_row[:], 0.0)
         w_scales = consts.tile([P, PASSES, D_OUT], U8, align_bytes=64)
         nc.vector.memset(w_scales[:].bitcast(I32), 0)
-        ones = consts.tile([P, P], BF16)
-        nc.vector.memset(ones[:], 1.0)
         table_warmer = consts.tile([P, 1], F32)
         nc.vector.memset(table_warmer[:], 0.0)
         identity = consts.tile([P, P], F32)
@@ -167,6 +170,10 @@ def tile_candidateaware_clickednewsattention_pa_t_kernel(
             nc.gpsimd.tensor_tensor(
                 out=norm_columns[:, b : b + 1], in0=square_sums[:, b : b + 1], in1=one_half[:], op=ALU.pow
             )
+
+        idle_work = acc_psum.tile([P, BANK], F32, tag="acc")
+        for i in range(WARMING_MATMULS):
+            nc.tensor.matmul(out=idle_work[:], lhsT=ones[:], rhs=zeros[:], start=True, stop=True)
 
         for b in range(ROUND):
             transpose_tile(b)

@@ -191,7 +191,27 @@ def tile_candidateaware_clickednewsattention_pa_t_kernel(
                     quantise_tile(b + ROUND)
             for b in range(first + 2 * ROUND, min(first + 3 * ROUND, USERS)):
                 transpose_tile(b)
-        norm_tile(USERS - 1)
+        last = USERS - 1
+        half_sums = consts.tile([P, BANKS_PER_USER], F32)
+        vector_squares = consts.tile([P, BANK], F32)
+        nc.scalar.activation(
+            out=squares[:, :BANK], in_=q_tiles[last][:, :BANK], func=ACT.Square, accum_out=half_sums[:, 0:1]
+        )
+        nc.vector.scalar_tensor_tensor(
+            out=vector_squares[:],
+            in0=q_tiles[last][:, BANK:],
+            scalar=1.0,
+            in1=q_tiles[last][:, BANK:],
+            op0=ALU.mult,
+            op1=ALU.mult,
+            accum_out=half_sums[:, 1:2],
+        )
+        nc.vector.tensor_tensor(
+            out=square_sums[:, last : last + 1], in0=half_sums[:, 0:1], in1=half_sums[:, 1:2], op=ALU.add
+        )
+        nc.gpsimd.tensor_tensor(
+            out=norm_columns[:, last : last + 1], in0=square_sums[:, last : last + 1], in1=one_half[:], op=ALU.pow
+        )
 
         norms = xt_psum.tile([P, P], F32, tag="xt")
         nc.tensor.transpose(norms[:], norm_columns[:], identity[:])

@@ -33,6 +33,7 @@ ROUND = 2
 VECTOR_COPY_EVERY = 4
 Q_TILES = 16
 WARMING_MATMULS = 4
+POW_FROM = USERS - 2
 
 FLOPS = 2 * USERS * P * D_IN * D_OUT
 
@@ -69,7 +70,7 @@ def tile_candidateaware_clickednewsattention_pa_t_kernel(
         square_sums = consts.tile([P, USERS], F32)
 
         nc.scalar.dma_start(out=bias_row[0:1, :], in_=bq.rearrange("(o f) -> o f", o=1))
-        nc.scalar.activation(out=table_warmer[:], in_=table_warmer[:], func=ACT.Exp)
+        nc.scalar.activation(out=table_warmer[:], in_=table_warmer[:], func=ACT.Sqrt)
 
         x_tiles = []
         for b in range(USERS):
@@ -167,9 +168,10 @@ def tile_candidateaware_clickednewsattention_pa_t_kernel(
             nc.scalar.activation(
                 out=squares[:], in_=q_tiles[b][:], func=ACT.Square, accum_out=square_sums[:, b : b + 1]
             )
-            nc.gpsimd.tensor_tensor(
-                out=norm_columns[:, b : b + 1], in0=square_sums[:, b : b + 1], in1=one_half[:], op=ALU.pow
-            )
+            if b >= POW_FROM:
+                nc.gpsimd.tensor_tensor(
+                    out=norm_columns[:, b : b + 1], in0=square_sums[:, b : b + 1], in1=one_half[:], op=ALU.pow
+                )
 
         idle_work = acc_psum.tile([P, BANK], F32, tag="acc")
         for i in range(WARMING_MATMULS):
@@ -197,6 +199,8 @@ def tile_candidateaware_clickednewsattention_pa_t_kernel(
         nc.scalar.activation(
             out=squares[:, :BANK], in_=q_tiles[last][:, :BANK], func=ACT.Square, accum_out=half_sums[:, 0:1]
         )
+        nc.scalar.activation(out=norm_columns[:, :POW_FROM], in_=square_sums[:, :POW_FROM], func=ACT.Sqrt)
+        nc.scalar.activation(out=table_warmer[:], in_=table_warmer[:], func=ACT.Exp)
         nc.vector.scalar_tensor_tensor(
             out=vector_squares[:],
             in0=q_tiles[last][:, BANK:],

@@ -34,6 +34,7 @@ VECTOR_COPY_EVERY = 4
 Q_TILES = 16
 WARMING_MATMULS = 4
 POW_FROM = USERS - 2
+SORT_AHEAD = 2 * ROUND
 
 FLOPS = 2 * USERS * P * D_IN * D_OUT
 
@@ -48,6 +49,7 @@ def tile_candidateaware_clickednewsattention_pa_t_kernel(
         x_pool = ctx.enter_context(tc.tile_pool(name="x_pool", bufs=1))
         mx_pool = ctx.enter_context(tc.tile_pool(name="mx_pool", bufs=2 * ROUND))
         q_pool = ctx.enter_context(tc.tile_pool(name="q_pool", bufs=Q_TILES))
+        sorted_pool = ctx.enter_context(tc.tile_pool(name="sorted_pool", bufs=SORT_AHEAD + ROUND))
         xt_psum = ctx.enter_context(tc.psum_pool(name="xt_psum", bufs=ROUND))
         acc_psum = ctx.enter_context(tc.psum_pool(name="acc_psum", bufs=PSUM_BANKS - ROUND))
 
@@ -114,16 +116,26 @@ def tile_candidateaware_clickednewsattention_pa_t_kernel(
         x_operands = {}
         q_tiles = {}
 
+        sorted_tiles = {}
+
+        def sort_tile(b):
+            sorted_tile = sorted_pool.tile([P, PASSES, PAIRS_PER_WORD, P], I32, align_bytes=64)
+            nc.gpsimd.tensor_copy(
+                out=sorted_tile[:],
+                in_=x_tiles[b][:].bitcast(I32).rearrange("n (g p u) -> n g u p", g=PASSES, u=PAIRS_PER_WORD),
+            )
+            sorted_tiles[b] = sorted_tile
+
         def transpose_tile(b):
             pairs = x_tiles[b][:].bitcast(F32)
             xt = xt_psum.tile([P, PASSES, PAIRS_PER_WORD, P], F32)
             for g in range(PASSES):
                 for u in range(PAIRS_PER_WORD):
-                    nc.tensor.transpose(
-                        xt[:, g, u, :],
-                        pairs[:, PAIRS_PER_PASS * g + u : PAIRS_PER_PASS * (g + 1) : PAIRS_PER_WORD],
-                        identity[:],
-                    )
+                    if b in sorted_tiles:
+                        in_ = sorted_tiles[b][:, g, u, :].bitcast(F32)
+                    else:
+                        in_ = pairs[:, PAIRS_PER_PASS * g + u : PAIRS_PER_PASS * (g + 1) : PAIRS_PER_WORD]
+                    nc.tensor.transpose(xt[:, g, u, :], in_, identity[:])
             grouped = mx_pool.tile([P, PASSES, P, PACK], BF16, align_bytes=64)
             pairs_side_by_side = xt[:].rearrange("p g u n -> p g n u")
             if b % VECTOR_COPY_EVERY == VECTOR_COPY_EVERY - 1:
@@ -183,6 +195,8 @@ def tile_candidateaware_clickednewsattention_pa_t_kernel(
             quantise_tile(b)
         for b in range(ROUND, 2 * ROUND):
             transpose_tile(b)
+        for b in range(2 * ROUND, 2 * ROUND + SORT_AHEAD):
+            sort_tile(b)
         spread_bias()
         for first in range(0, USERS, ROUND):
             for b in range(first, first + ROUND):
@@ -193,6 +207,8 @@ def tile_candidateaware_clickednewsattention_pa_t_kernel(
                     quantise_tile(b + ROUND)
             for b in range(first + 2 * ROUND, min(first + 3 * ROUND, USERS)):
                 transpose_tile(b)
+            for b in range(first + 2 * ROUND + SORT_AHEAD, min(first + 3 * ROUND + SORT_AHEAD, USERS)):
+                sort_tile(b)
         last = USERS - 1
         half_sums = consts.tile([P, BANKS_PER_USER], F32)
         vector_squares = consts.tile([P, BANK], F32)

@@ -34,7 +34,6 @@ VECTOR_COPY_EVERY = 4
 Q_TILES = 16
 WARMING_MATMULS = 4
 POW_FROM = USERS - 2
-SORT_AHEAD = 2 * ROUND
 
 FLOPS = 2 * USERS * P * D_IN * D_OUT
 
@@ -49,7 +48,6 @@ def tile_candidateaware_clickednewsattention_pa_t_kernel(
         x_pool = ctx.enter_context(tc.tile_pool(name="x_pool", bufs=1))
         mx_pool = ctx.enter_context(tc.tile_pool(name="mx_pool", bufs=2 * ROUND))
         q_pool = ctx.enter_context(tc.tile_pool(name="q_pool", bufs=Q_TILES))
-        sorted_pool = ctx.enter_context(tc.tile_pool(name="sorted_pool", bufs=SORT_AHEAD + ROUND))
         xt_psum = ctx.enter_context(tc.psum_pool(name="xt_psum", bufs=ROUND))
         acc_psum = ctx.enter_context(tc.psum_pool(name="acc_psum", bufs=PSUM_BANKS - ROUND))
 
@@ -116,33 +114,37 @@ def tile_candidateaware_clickednewsattention_pa_t_kernel(
         x_operands = {}
         q_tiles = {}
 
-        sorted_tiles = {}
-
         def sort_tile(b):
-            sorted_tile = sorted_pool.tile([P, PASSES, PAIRS_PER_WORD, P], I32, align_bytes=64)
+            grouped = mx_pool.tile([P, PASSES, P, PACK], BF16, align_bytes=64)
             nc.gpsimd.tensor_copy(
-                out=sorted_tile[:],
+                out=grouped[:].rearrange("n g p t -> n (g p t)").bitcast(I32).rearrange(
+                    "n (g u p) -> n g u p", g=PASSES, u=PAIRS_PER_WORD
+                ),
                 in_=x_tiles[b][:].bitcast(I32).rearrange("n (g p u) -> n g u p", g=PASSES, u=PAIRS_PER_WORD),
             )
-            sorted_tiles[b] = sorted_tile
+            grouped_tiles[b] = grouped
 
         def transpose_tile(b):
             pairs = x_tiles[b][:].bitcast(F32)
+            if b in grouped_tiles:
+                sorted_pairs = grouped_tiles[b][:].rearrange("n g p t -> n (g p t)").bitcast(F32)
             xt = xt_psum.tile([P, PASSES, PAIRS_PER_WORD, P], F32)
             for g in range(PASSES):
                 for u in range(PAIRS_PER_WORD):
-                    if b in sorted_tiles:
-                        in_ = sorted_tiles[b][:, g, u, :].bitcast(F32)
+                    if b in grouped_tiles:
+                        run = P * (PAIRS_PER_WORD * g + u)
+                        in_ = sorted_pairs[:, run : run + P]
                     else:
                         in_ = pairs[:, PAIRS_PER_PASS * g + u : PAIRS_PER_PASS * (g + 1) : PAIRS_PER_WORD]
                     nc.tensor.transpose(xt[:, g, u, :], in_, identity[:])
-            grouped = mx_pool.tile([P, PASSES, P, PACK], BF16, align_bytes=64)
+            if b not in grouped_tiles:
+                grouped_tiles[b] = mx_pool.tile([P, PASSES, P, PACK], BF16, name="grouped", align_bytes=64)
+            grouped = grouped_tiles[b]
             pairs_side_by_side = xt[:].rearrange("p g u n -> p g n u")
             if b % VECTOR_COPY_EVERY == VECTOR_COPY_EVERY - 1:
                 nc.vector.tensor_copy(out=grouped[:].bitcast(F32), in_=pairs_side_by_side)
             else:
                 nc.scalar.copy(out=grouped[:].bitcast(F32), in_=pairs_side_by_side)
-            grouped_tiles[b] = grouped
 
         def quantise_tile(b):
             x_codes = mx_pool.tile([P, PASSES * P], U32, align_bytes=64)
@@ -153,6 +155,8 @@ def tile_candidateaware_clickednewsattention_pa_t_kernel(
                 in_=grouped_tiles[b][:].rearrange("p g n t -> p (g n t)"),
             )
             x_operands[b] = (x_codes, x_scales)
+            if b + 2 * ROUND < USERS:
+                sort_tile(b + 2 * ROUND)
 
         def project_tile(b):
             x_codes, x_scales = x_operands[b]
@@ -195,8 +199,6 @@ def tile_candidateaware_clickednewsattention_pa_t_kernel(
             quantise_tile(b)
         for b in range(ROUND, 2 * ROUND):
             transpose_tile(b)
-        for b in range(2 * ROUND, 2 * ROUND + SORT_AHEAD):
-            sort_tile(b)
         spread_bias()
         for first in range(0, USERS, ROUND):
             for b in range(first, first + ROUND):
@@ -207,8 +209,6 @@ def tile_candidateaware_clickednewsattention_pa_t_kernel(
                     quantise_tile(b + ROUND)
             for b in range(first + 2 * ROUND, min(first + 3 * ROUND, USERS)):
                 transpose_tile(b)
-            for b in range(first + 2 * ROUND + SORT_AHEAD, min(first + 3 * ROUND + SORT_AHEAD, USERS)):
-                sort_tile(b)
         last = USERS - 1
         half_sums = consts.tile([P, BANKS_PER_USER], F32)
         vector_squares = consts.tile([P, BANK], F32)

@@ -32,8 +32,9 @@ SCALE_ROWS = QUADRANT // 8
 ROUND = 2
 VECTOR_COPY_EVERY = 4
 Q_TILES = 16
-WARMING_MATMULS = 4
+WARMING_MATMULS = 2
 POW_FROM = USERS - 2
+XT_BANKS = 4
 
 FLOPS = 2 * USERS * P * D_IN * D_OUT
 
@@ -48,8 +49,8 @@ def tile_candidateaware_clickednewsattention_pa_t_kernel(
         x_pool = ctx.enter_context(tc.tile_pool(name="x_pool", bufs=1))
         mx_pool = ctx.enter_context(tc.tile_pool(name="mx_pool", bufs=2 * ROUND))
         q_pool = ctx.enter_context(tc.tile_pool(name="q_pool", bufs=Q_TILES))
-        xt_psum = ctx.enter_context(tc.psum_pool(name="xt_psum", bufs=ROUND))
-        acc_psum = ctx.enter_context(tc.psum_pool(name="acc_psum", bufs=PSUM_BANKS - ROUND))
+        xt_psum = ctx.enter_context(tc.psum_pool(name="xt_psum", bufs=XT_BANKS))
+        acc_psum = ctx.enter_context(tc.psum_pool(name="acc_psum", bufs=PSUM_BANKS - XT_BANKS))
 
         ones = consts.tile([P, P], BF16)
         nc.vector.memset(ones[:], 1.0)
@@ -108,7 +109,7 @@ def tile_candidateaware_clickednewsattention_pa_t_kernel(
                 nc.tensor.matmul(
                     out=acc[:], lhsT=ones[:], rhs=bias_row[:, BANK * h : BANK * (h + 1)], start=True, stop=True
                 )
-                nc.vector.tensor_copy(out=bias[:, BANK * h : BANK * (h + 1)], in_=acc[:])
+                nc.scalar.copy(out=bias[:, BANK * h : BANK * (h + 1)], in_=acc[:])
 
         grouped_tiles = {}
         x_operands = {}
@@ -123,6 +124,11 @@ def tile_candidateaware_clickednewsattention_pa_t_kernel(
                 in_=x_tiles[b][:].bitcast(I32).rearrange("n (g p u) -> n g u p", g=PASSES, u=PAIRS_PER_WORD),
             )
             grouped_tiles[b] = grouped
+
+        def vector_copies(b):
+            if b < 2 * ROUND:
+                return b % 2 == 1
+            return b % VECTOR_COPY_EVERY == VECTOR_COPY_EVERY - 1
 
         def transpose_tile(b):
             pairs = x_tiles[b][:].bitcast(F32)
@@ -141,7 +147,7 @@ def tile_candidateaware_clickednewsattention_pa_t_kernel(
                 grouped_tiles[b] = mx_pool.tile([P, PASSES, P, PACK], BF16, name="grouped", align_bytes=64)
             grouped = grouped_tiles[b]
             pairs_side_by_side = xt[:].rearrange("p g u n -> p g n u")
-            if b % VECTOR_COPY_EVERY == VECTOR_COPY_EVERY - 1:
+            if vector_copies(b):
                 nc.vector.tensor_copy(out=grouped[:].bitcast(F32), in_=pairs_side_by_side)
             else:
                 nc.scalar.copy(out=grouped[:].bitcast(F32), in_=pairs_side_by_side)
@@ -197,9 +203,9 @@ def tile_candidateaware_clickednewsattention_pa_t_kernel(
             transpose_tile(b)
         for b in range(ROUND):
             quantise_tile(b)
+        spread_bias()
         for b in range(ROUND, 2 * ROUND):
             transpose_tile(b)
-        spread_bias()
         for first in range(0, USERS, ROUND):
             for b in range(first, first + ROUND):
                 project_tile(b)

@@ -30,11 +30,13 @@ QUADRANTS = P // QUADRANT
 SCALE_ROWS = QUADRANT // 8
 
 ROUND = 2
-VECTOR_COPY_EVERY = 4
 Q_TILES = 16
 WARMING_MATMULS = 2
 POW_FROM = USERS - 2
 XT_BANKS = 4
+SPLIT = 448
+REST = SPLIT // 4
+LAST_SPLIT = 28
 
 FLOPS = 2 * USERS * P * D_IN * D_OUT
 
@@ -49,6 +51,8 @@ def tile_candidateaware_clickednewsattention_pa_t_kernel(
         x_pool = ctx.enter_context(tc.tile_pool(name="x_pool", bufs=1))
         mx_pool = ctx.enter_context(tc.tile_pool(name="mx_pool", bufs=2 * ROUND))
         q_pool = ctx.enter_context(tc.tile_pool(name="q_pool", bufs=Q_TILES))
+        gp_pool = ctx.enter_context(tc.tile_pool(name="gp_pool", bufs=2))
+        rest_pool = ctx.enter_context(tc.tile_pool(name="rest_pool", bufs=4))
         xt_psum = ctx.enter_context(tc.psum_pool(name="xt_psum", bufs=XT_BANKS))
         acc_psum = ctx.enter_context(tc.psum_pool(name="acc_psum", bufs=PSUM_BANKS - XT_BANKS))
 
@@ -115,37 +119,21 @@ def tile_candidateaware_clickednewsattention_pa_t_kernel(
         x_operands = {}
         q_tiles = {}
 
-        def sort_tile(b):
-            grouped = mx_pool.tile([P, PASSES, P, PACK], BF16, align_bytes=64)
-            nc.gpsimd.tensor_copy(
-                out=grouped[:].rearrange("n g p t -> n (g p t)").bitcast(I32).rearrange(
-                    "n (g u p) -> n g u p", g=PASSES, u=PAIRS_PER_WORD
-                ),
-                in_=x_tiles[b][:].bitcast(I32).rearrange("n (g p u) -> n g u p", g=PASSES, u=PAIRS_PER_WORD),
-            )
-            grouped_tiles[b] = grouped
-
         def vector_copies(b):
-            if b < 2 * ROUND:
-                return b % 2 == 1
-            return b % VECTOR_COPY_EVERY == VECTOR_COPY_EVERY - 1
+            return b < 2 * ROUND and b % 2 == 1
 
         def transpose_tile(b):
             pairs = x_tiles[b][:].bitcast(F32)
-            if b in grouped_tiles:
-                sorted_pairs = grouped_tiles[b][:].rearrange("n g p t -> n (g p t)").bitcast(F32)
             xt = xt_psum.tile([P, PASSES, PAIRS_PER_WORD, P], F32)
             for g in range(PASSES):
                 for u in range(PAIRS_PER_WORD):
-                    if b in grouped_tiles:
-                        run = P * (PAIRS_PER_WORD * g + u)
-                        in_ = sorted_pairs[:, run : run + P]
-                    else:
-                        in_ = pairs[:, PAIRS_PER_PASS * g + u : PAIRS_PER_PASS * (g + 1) : PAIRS_PER_WORD]
-                    nc.tensor.transpose(xt[:, g, u, :], in_, identity[:])
-            if b not in grouped_tiles:
-                grouped_tiles[b] = mx_pool.tile([P, PASSES, P, PACK], BF16, name="grouped", align_bytes=64)
-            grouped = grouped_tiles[b]
+                    nc.tensor.transpose(
+                        xt[:, g, u, :],
+                        pairs[:, PAIRS_PER_PASS * g + u : PAIRS_PER_PASS * (g + 1) : PAIRS_PER_WORD],
+                        identity[:],
+                    )
+            grouped = mx_pool.tile([P, PASSES, P, PACK], BF16, align_bytes=64)
+            grouped_tiles[b] = grouped
             pairs_side_by_side = xt[:].rearrange("p g u n -> p g n u")
             if vector_copies(b):
                 nc.vector.tensor_copy(out=grouped[:].bitcast(F32), in_=pairs_side_by_side)
@@ -161,8 +149,6 @@ def tile_candidateaware_clickednewsattention_pa_t_kernel(
                 in_=grouped_tiles[b][:].rearrange("p g n t -> p (g n t)"),
             )
             x_operands[b] = (x_codes, x_scales)
-            if b + 2 * ROUND < USERS:
-                sort_tile(b + 2 * ROUND)
 
         def project_tile(b):
             x_codes, x_scales = x_operands[b]
@@ -195,6 +181,24 @@ def tile_candidateaware_clickednewsattention_pa_t_kernel(
                     out=norm_columns[:, b : b + 1], in0=square_sums[:, b : b + 1], in1=one_half[:], op=ALU.pow
                 )
 
+        rest_tiles = {}
+
+        def split_norm(b):
+            own = D_OUT - SPLIT
+            rest = rest_pool.tile([P, REST + 1], F32)
+            nc.scalar.activation(
+                out=squares[:, :own], in_=q_tiles[b][:, :own], func=ACT.Square, accum_out=rest[:, REST:]
+            )
+            wide = gp_pool.tile([P, SPLIT], F32)
+            nc.gpsimd.tensor_tensor(out=wide[:], in0=q_tiles[b][:, own:], in1=q_tiles[b][:, own:], op=ALU.mult)
+            half = gp_pool.tile([P, SPLIT // 2], F32)
+            nc.gpsimd.tensor_tensor(out=half[:], in0=wide[:, : SPLIT // 2], in1=wide[:, SPLIT // 2 :], op=ALU.add)
+            nc.gpsimd.tensor_tensor(out=rest[:, :REST], in0=half[:, :REST], in1=half[:, REST:], op=ALU.add)
+            rest_tiles[b] = rest
+
+        def finish_norm(b):
+            nc.vector.tensor_reduce(out=square_sums[:, b : b + 1], in_=rest_tiles[b][:], axis=AXIS.X, op=ALU.add)
+
         idle_work = acc_psum.tile([P, BANK], F32, tag="acc")
         for i in range(WARMING_MATMULS):
             nc.tensor.matmul(out=idle_work[:], lhsT=ones[:], rhs=zeros[:], start=True, stop=True)
@@ -210,9 +214,14 @@ def tile_candidateaware_clickednewsattention_pa_t_kernel(
             for b in range(first, first + ROUND):
                 project_tile(b)
                 if b > 0:
-                    norm_tile(b - 1)
+                    if (b - 1) % 2 == 0 and b - 1 <= LAST_SPLIT:
+                        split_norm(b - 1)
+                    else:
+                        norm_tile(b - 1)
                 if b + ROUND < USERS:
                     quantise_tile(b + ROUND)
+                if b - 3 in rest_tiles:
+                    finish_norm(b - 3)
             for b in range(first + 2 * ROUND, min(first + 3 * ROUND, USERS)):
                 transpose_tile(b)
         last = USERS - 1

from contextlib import ExitStack

import concourse.mybir as mybir
from concourse.masks import make_identity

F32 = mybir.dt.float32
BF16 = mybir.dt.bfloat16
I32 = mybir.dt.int32
U32 = mybir.dt.uint32
U8 = mybir.dt.uint8
FP8X4 = mybir.dt.float8_e4m3fn_x4
ACT = mybir.ActivationFunctionType
ALU = mybir.AluOpType
AXIS = mybir.AxisListType

P = 128
USERS = 32
D_IN = 1024
D_OUT = 1024
PACK = 4
K_PASS = P * PACK
PASSES = D_IN // K_PASS
PAIRS_PER_WORD = PACK // 2
PAIRS_PER_PASS = K_PASS // 2
BANK = 512
BANKS_PER_USER = D_OUT // BANK
PSUM_BANKS = 8
QUADRANT = 32
QUADRANTS = P // QUADRANT
SCALE_ROWS = QUADRANT // 8

ROUND = 2
Q_TILES = 16
WARMING_MATMULS = 2
POW_FROM = USERS - 2
XT_BANKS = 4
SPLIT = 448
REST = SPLIT // 4
LAST_SPLIT = 28

FLOPS = 2 * USERS * P * D_IN * D_OUT


def tile_candidateaware_clickednewsattention_pa_t_kernel(
    tc, cand_topics, Wq_words, Wq_scales, bq, out_0, out_1
):
    nc = tc.nc
    with ExitStack() as ctx:
        ctx.enter_context(tc.manual_schedule())
        consts = ctx.enter_context(tc.tile_pool(name="consts", bufs=1))
        x_pool = ctx.enter_context(tc.tile_pool(name="x_pool", bufs=1))
        mx_pool = ctx.enter_context(tc.tile_pool(name="mx_pool", bufs=2 * ROUND))
        q_pool = ctx.enter_context(tc.tile_pool(name="q_pool", bufs=Q_TILES))
        gp_pool = ctx.enter_context(tc.tile_pool(name="gp_pool", bufs=2))
        rest_pool = ctx.enter_context(tc.tile_pool(name="rest_pool", bufs=4))
        xt_psum = ctx.enter_context(tc.psum_pool(name="xt_psum", bufs=XT_BANKS))
        acc_psum = ctx.enter_context(tc.psum_pool(name="acc_psum", bufs=PSUM_BANKS - XT_BANKS))

        ones = consts.tile([P, P], BF16)
        nc.vector.memset(ones[:], 1.0)
        zeros = consts.tile([P, BANK], BF16)
        nc.vector.memset(zeros[:], 0.0)
        bias_row = consts.tile([P, D_OUT], BF16)
        nc.vector.memset(bias_row[:], 0.0)
        w_scales = consts.tile([P, PASSES, D_OUT], U8, align_bytes=64)
        nc.vector.memset(w_scales[:].bitcast(I32), 0)
        table_warmer = consts.tile([P, 1], F32)
        nc.vector.memset(table_warmer[:], 0.0)
        identity = consts.tile([P, P], F32)
        make_identity(nc, identity[:])
        norm_columns = consts.tile([P, P], F32)
        nc.gpsimd.memset(norm_columns[:], 0.0)
        one_half = consts.tile([P, 1], F32)
        nc.gpsimd.memset(one_half[:], 0.5)
        square_sums = consts.tile([P, USERS], F32)

        nc.scalar.dma_start(out=bias_row[0:1, :], in_=bq.rearrange("(o f) -> o f", o=1))
        nc.scalar.activation(out=table_warmer[:], in_=table_warmer[:], func=ACT.Sqrt)

        x_tiles = []
        for b in range(USERS):
            x_tile = x_pool.tile([P, D_IN], BF16, name="x_tile%d" % b)
            x_tiles.append(x_tile)

        def load_x(b):
            nc.sync.dma_start(out=x_tiles[b][:], in_=cand_topics[b])

        for b in range(2 * ROUND):
            load_x(b)
        for quadrant in range(QUADRANTS):
            nc.sync.dma_start(
                out=w_scales[QUADRANT * quadrant : QUADRANT * quadrant + SCALE_ROWS, :, :].bitcast(I32),
                in_=Wq_scales[:, SCALE_ROWS * quadrant : SCALE_ROWS * (quadrant + 1), :]
                .rearrange("g r f -> r g f")
                .bitcast(I32),
            )
        w_codes = consts.tile([P, PASSES, PACK * D_OUT], U8, align_bytes=64)
        w_bytes = Wq_words.rearrange("g p f t -> p g (f t)")
        for h in range(BANKS_PER_USER):
            bank_bytes = slice(PACK * BANK * h, PACK * BANK * (h + 1))
            nc.sync.dma_start(
                out=w_codes[:, :, bank_bytes].bitcast(I32),
                in_=w_bytes[:, :, bank_bytes].bitcast(I32),
            )
        for b in range(2 * ROUND, USERS):
            load_x(b)

        bias = consts.tile([P, D_OUT], F32)

        def spread_bias():
            for h in range(BANKS_PER_USER):
                acc = acc_psum.tile([P, BANK], F32)
                nc.tensor.matmul(
                    out=acc[:], lhsT=ones[:], rhs=bias_row[:, BANK * h : BANK * (h + 1)], start=True, stop=True
                )
                nc.scalar.copy(out=bias[:, BANK * h : BANK * (h + 1)], in_=acc[:])

        grouped_tiles = {}
        x_operands = {}
        q_tiles = {}

        def vector_copies(b):
            return b < 2 * ROUND and b % 2 == 1

        def transpose_tile(b):
            pairs = x_tiles[b][:].bitcast(F32)
            xt = xt_psum.tile([P, PASSES, PAIRS_PER_WORD, P], F32)
            for g in range(PASSES):
                for u in range(PAIRS_PER_WORD):
                    nc.tensor.transpose(
                        xt[:, g, u, :],
                        pairs[:, PAIRS_PER_PASS * g + u : PAIRS_PER_PASS * (g + 1) : PAIRS_PER_WORD],
                        identity[:],
                    )
            grouped = mx_pool.tile([P, PASSES, P, PACK], BF16, align_bytes=64)
            grouped_tiles[b] = grouped
            pairs_side_by_side = xt[:].rearrange("p g u n -> p g n u")
            if vector_copies(b):
                nc.vector.tensor_copy(out=grouped[:].bitcast(F32), in_=pairs_side_by_side)
            else:
                nc.scalar.copy(out=grouped[:].bitcast(F32), in_=pairs_side_by_side)

        def quantise_tile(b):
            x_codes = mx_pool.tile([P, PASSES * P], U32, align_bytes=64)
            x_scales = mx_pool.tile([P, PASSES * P], U8, align_bytes=64)
            nc.vector.quantize_mx(
                out=x_codes[:].bitcast(FP8X4),
                scales=x_scales[:],
                in_=grouped_tiles[b][:].rearrange("p g n t -> p (g n t)"),
            )
            x_operands[b] = (x_codes, x_scales)

        def project_tile(b):
            x_codes, x_scales = x_operands[b]
            q_tile = q_pool.tile([P, D_OUT], F32)
            for h in range(BANKS_PER_USER):
                acc = acc_psum.tile([P, BANK], F32)
                for g in range(PASSES):
                    nc.tensor.matmul_mx(
                        out=acc[:],
                        lhsT=x_codes[:, P * g : P * (g + 1)].bitcast(FP8X4),
                        lhsT_scale=x_scales[:, P * g : P * (g + 1)],
                        rhs=w_codes[:, g, PACK * BANK * h : PACK * BANK * (h + 1)].bitcast(FP8X4),
                        rhs_scale=w_scales[:, g, BANK * h : BANK * (h + 1)],
                        start=(g == 0),
                        stop=(g == PASSES - 1),
                    )
                features = slice(BANK * h, BANK * (h + 1))
                nc.vector.tensor_tensor(out=q_tile[:, features], in0=acc[:], in1=bias[:, features], op=ALU.add)
            nc.sync.dma_start(out=out_0[b], in_=q_tile[:])
            q_tiles[b] = q_tile

        squares = consts.tile([P, D_OUT], F32)

        def norm_tile(b):
            nc.scalar.activation(
                out=squares[:], in_=q_tiles[b][:], func=ACT.Square, accum_out=square_sums[:, b : b + 1]
            )
            if b >= POW_FROM:
                nc.gpsimd.tensor_tensor(
                    out=norm_columns[:, b : b + 1], in0=square_sums[:, b : b + 1], in1=one_half[:], op=ALU.pow
                )

        rest_tiles = {}

        def split_norm(b):
            own = D_OUT - SPLIT
            rest = rest_pool.tile([P, REST + 1], F32)
            nc.scalar.activation(
                out=squares[:, :own], in_=q_tiles[b][:, :own], func=ACT.Square, accum_out=rest[:, REST:]
            )
            wide = gp_pool.tile([P, SPLIT], F32)
            nc.gpsimd.tensor_tensor(out=wide[:], in0=q_tiles[b][:, own:], in1=q_tiles[b][:, own:], op=ALU.mult)
            half = gp_pool.tile([P, SPLIT // 2], F32)
            nc.gpsimd.tensor_tensor(out=half[:], in0=wide[:, : SPLIT // 2], in1=wide[:, SPLIT // 2 :], op=ALU.add)
            nc.gpsimd.tensor_tensor(out=rest[:, :REST], in0=half[:, :REST], in1=half[:, REST:], op=ALU.add)
            rest_tiles[b] = rest

        def finish_norm(b):
            nc.vector.tensor_reduce(out=square_sums[:, b : b + 1], in_=rest_tiles[b][:], axis=AXIS.X, op=ALU.add)

        idle_work = acc_psum.tile([P, BANK], F32, tag="acc")
        for i in range(WARMING_MATMULS):
            nc.tensor.matmul(out=idle_work[:], lhsT=ones[:], rhs=zeros[:], start=True, stop=True)

        for b in range(ROUND):
            transpose_tile(b)
        for b in range(ROUND):
            quantise_tile(b)
        spread_bias()
        for b in range(ROUND, 2 * ROUND):
            transpose_tile(b)
        for first in range(0, USERS, ROUND):
            for b in range(first, first + ROUND):
                project_tile(b)
                if b > 0:
                    if (b - 1) % 2 == 0 and b - 1 <= LAST_SPLIT:
                        split_norm(b - 1)
                    else:
                        norm_tile(b - 1)
                if b + ROUND < USERS:
                    quantise_tile(b + ROUND)
                if b - 3 in rest_tiles:
                    finish_norm(b - 3)
            for b in range(first + 2 * ROUND, min(first + 3 * ROUND, USERS)):
                transpose_tile(b)
        last = USERS - 1
        half_sums = consts.tile([P, BANKS_PER_USER], F32)
        vector_squares = consts.tile([P, BANK], F32)
        nc.scalar.activation(
            out=squares[:, :BANK], in_=q_tiles[last][:, :BANK], func=ACT.Square, accum_out=half_sums[:, 0:1]
        )
        nc.scalar.activation(out=norm_columns[:, :POW_FROM], in_=square_sums[:, :POW_FROM], func=ACT.Sqrt)
        nc.scalar.activation(out=table_warmer[:], in_=table_warmer[:], func=ACT.Exp)
        nc.vector.scalar_tensor_tensor(
            out=vector_squares[:],
            in0=q_tiles[last][:, BANK:],
            scalar=1.0,
            in1=q_tiles[last][:, BANK:],
            op0=ALU.mult,
            op1=ALU.mult,
            accum_out=half_sums[:, 1:2],
        )
        nc.vector.tensor_tensor(
            out=square_sums[:, last : last + 1], in0=half_sums[:, 0:1], in1=half_sums[:, 1:2], op=ALU.add
        )
        nc.gpsimd.tensor_tensor(
            out=norm_columns[:, last : last + 1], in0=square_sums[:, last : last + 1], in1=one_half[:], op=ALU.pow
        )

        norms = xt_psum.tile([P, P], F32, tag="xt")
        nc.tensor.transpose(norms[:], norm_columns[:], identity[:])
        minus_max = consts.tile([P, 1], F32)
        nc.vector.tensor_reduce(out=minus_max[:USERS], in_=norms[:USERS], axis=AXIS.X, op=ALU.max, negate=True)
        exps = consts.tile([P, P], F32)
        exp_sum = consts.tile([P, 1], F32)
        nc.scalar.activation(
            out=exps[:USERS], in_=norms[:USERS], func=ACT.Exp, bias=minus_max[:USERS], accum_out=exp_sum[:USERS]
        )
        one_over_sum = consts.tile([P, 1], F32)
        nc.vector.reciprocal(out=one_over_sum[:USERS], in_=exp_sum[:USERS])
        query_weights = consts.tile([P, P], F32)
        nc.vector.tensor_scalar_mul(out=query_weights[:USERS], in0=exps[:USERS], scalar1=one_over_sum[:USERS])
        nc.sync.dma_start(out=out_1, in_=query_weights[:USERS])
